import numpy as np
import ml_dtypes


def mxq(x, axis, fmt="e4m3"):
    dtype, down = {"e4m3": (ml_dtypes.float8_e4m3fn, 7), "e5m2": (ml_dtypes.float8_e5m2, 14)}[fmt]
    v = np.moveaxis(np.asarray(x, np.float32).astype(ml_dtypes.bfloat16).astype(np.float64), axis, -1)
    blocks = v.reshape(v.shape[:-1] + (-1, 32))
    amax = np.abs(blocks).max(-1, keepdims=True)
    byte = np.maximum(np.where(amax > 0, np.frexp(amax)[1] - 1 + 127, 0) - down, 1)
    scale = np.exp2(byte - 127.0)
    codes = (blocks / scale).astype(np.float32).astype(dtype).astype(np.float64)
    return np.moveaxis((codes * scale).reshape(v.shape), -1, axis)


WIDE = False


def mx_kscale(k):
    if not WIDE:
        return np.ones(k)
    levels = np.array([10, -10, 5, -5, 0])
    if k % 512:
        return np.exp2(np.random.permutation(np.resize(levels, k // 32))).repeat(32)
    a = np.empty((k // 512, 16))
    for p in range(k // 512):
        a[p, :8] = np.random.permutation(np.resize(levels, 8))
        for g in range(8):
            far = levels[np.abs(levels - a[p, g]) >= 10]
            a[p, g + 8] = far[np.random.randint(len(far))]
    return np.exp2(a.ravel()).repeat(32)


BF16 = ml_dtypes.bfloat16


def bf(x):
    return np.asarray(x, np.float32).astype(BF16)


def f64(x):
    return np.asarray(x).astype(np.float64)


B, R, CIN, N_CAPS, COUT = 512, 576, 8, 32, 16
K = R * CIN
M = N_CAPS * COUT


def setup_inputs():
    t = mx_kscale(B)
    u = mx_kscale(M)[::COUT]
    x0 = bf(np.random.standard_normal((B, R, CIN)))
    W0 = bf(np.random.standard_normal((N_CAPS, R, CIN, COUT)) * np.sqrt(3.0 * R / (CIN * COUT)))
    g = bf(np.random.standard_normal((N_CAPS, B, 1, 1, COUT))
           * np.exp2(np.random.randint(-6, 1, (1, B, 1, 1, 1))) * float(R)
           / t[None, :, None, None, None] * u[:, None, None, None, None])
    s = (1.0 / R) * (f64(x0).reshape(B, K) @ f64(W0).reshape(N_CAPS, K, COUT))
    return {"x": bf(f64(x0) * t[:, None, None]), "W": bf(f64(W0) / u[:, None, None, None]),
            "s": np.asarray(s, np.float32), "grad_out": g}


def reference(x, W, s, grad_out):
    sf = f64(s)
    g = f64(grad_out).reshape(N_CAPS, B, COUT)
    sq = np.sum(sf * sf, axis=-1, keepdims=True)
    rt = np.sqrt(sq)
    dot = np.sum(g * sf, axis=-1, keepdims=True)
    ds = g * (rt / (1.0 + sq)) + sf * (dot * (1.0 - sq) / (rt * (1.0 + sq) ** 2))
    dsm = ds.transpose(1, 0, 2).reshape(B, M)
    xm = f64(x).reshape(B, K)
    wm = f64(W).transpose(1, 2, 0, 3).reshape(K, M)
    c = 1.0 / R
    dx = c * (mxq(dsm, 1, "e5m2") @ mxq(wm, 1, "e4m3").T)
    dw = c * (mxq(xm, 0, "e4m3").T @ mxq(dsm, 0, "e5m2"))
    return dx.reshape(B, R, CIN), dw.reshape(R, CIN, N_CAPS, COUT).transpose(2, 0, 1, 3)

@@ -1,0 +1,259 @@
+from contextlib import ExitStack
+
+import concourse.masks as masks
+import concourse.mybir as mybir
+
+FLOPS = 2 * 2 * 512 * 4608 * 512
+
+F32 = mybir.dt.float32
+BF16 = mybir.dt.bfloat16
+U32 = mybir.dt.uint32
+U8 = mybir.dt.uint8
+E4 = mybir.dt.float8_e4m3fn_x4
+E5 = mybir.dt.float8_e5m2_x4
+ALU = mybir.AluOpType
+ACT = mybir.ActivationFunctionType
+AX = mybir.AxisListType
+
+P = 128
+K = 4608
+KL = 18
+KCH = P * KL
+WKL = 36
+INV_R = 1.0 / 576.0
+UNITS = ((0, 4), (4, 8), (8, 12), (12, 16), (16, 18))
+
+S0, A0, B0, G0 = 0, 2048, 4096, 6144
+
+
+def tile_capsulelayer_v_kernel(tc, x, W, s, grad_out, out_0, out_1):
+    nc = tc.nc
+
+    xv = x.rearrange("(p j) r i -> p j (r i)", j=4)
+    wv = W.rearrange("n r i o -> n (r i o)").rearrange("n (kp f) -> kp n f", kp=P)
+    sv = s.rearrange("n (p j) o -> p n (j o)", j=4)
+    gv = grad_out.rearrange("n (p j) a c o -> p n (j a c o)", j=4)
+    o0v = out_0.rearrange("(p j) r i -> p j (r i)", j=4)
+    o1f = out_1.rearrange("n r i o -> n (r i o)")
+
+    with ExitStack() as ctx:
+        const = ctx.enter_context(tc.tile_pool(name="const", bufs=1))
+        big = ctx.enter_context(tc.tile_pool(name="big", bufs=4))
+        cod = ctx.enter_context(tc.tile_pool(name="cod", bufs=2))
+        wcod = ctx.enter_context(tc.tile_pool(name="wcod", bufs=3))
+        rot = ctx.enter_context(tc.tile_pool(name="rot", bufs=8))
+        psum = ctx.enter_context(tc.psum_pool(name="psum", bufs=8))
+
+        ident = const.tile([P, P], F32, name="ident", tag="ident")
+        masks.make_identity(nc, ident[:])
+        warm_in = const.tile([P, 8], F32, name="warm_in", tag="warm_in")
+        warm_out = const.tile([P, 8], F32, name="warm_out", tag="warm_out")
+        nc.vector.memset(warm_in[:], 1.0)
+        nc.scalar.activation(out=warm_out[:], in_=warm_in[:], func=ACT.Sqrt)
+
+        scr = big.tile([P, 9216], F32, name="scr", tag="big", align_bytes=64)
+        x_raw = big.tile([P, 4, K], BF16, name="x_raw", tag="big", align_bytes=64)
+        w_raw = big.tile([P, 32 * 576], BF16, name="w_raw", tag="big", align_bytes=64)
+        g_all = scr[:, G0 : G0 + 1024].bitcast(BF16)
+
+        def load_sg(h):
+            nc.sync.dma_start(
+                out=scr[:, S0 + 1024 * h : S0 + 1024 * (h + 1)].rearrange("p (n f) -> p n f", f=64),
+                in_=sv[:, 16 * h : 16 * (h + 1), :],
+            )
+            nc.sync.dma_start(
+                out=g_all[:, 1024 * h : 1024 * (h + 1)].rearrange("p (n f) -> p n f", f=64),
+                in_=gv[:, 16 * h : 16 * (h + 1), :],
+            )
+
+        def load_x(c):
+            nc.sync.dma_start(out=x_raw[:, :, KCH * c : KCH * (c + 1)], in_=xv[:, :, KCH * c : KCH * (c + 1)])
+
+        load_sg(0)
+        load_x(0)
+        load_sg(1)
+        load_x(1)
+        for q in range(4):
+            nc.sync.dma_start(
+                out=w_raw[:, 576 * 8 * q : 576 * 8 * (q + 1)].rearrange("p (n f) -> p n f", f=576),
+                in_=wv[:, 8 * q : 8 * (q + 1), :],
+            )
+
+        sq = const.tile([P, P], F32, name="sq", tag="sq")
+        dot = const.tile([P, P], F32, name="dot", tag="dot")
+        rt = const.tile([P, P], F32, name="rt", tag="rt")
+        onep = const.tile([P, P], F32, name="onep", tag="onep")
+        inv = const.tile([P, P], F32, name="inv", tag="inv")
+        rinv = const.tile([P, P], F32, name="rinv", tag="rinv")
+        ca = const.tile([P, P], F32, name="ca", tag="ca")
+        u1 = const.tile([P, P], F32, name="u1", tag="u1")
+        u2 = const.tile([P, P], F32, name="u2", tag="u2")
+        u3 = const.tile([P, P], F32, name="u3", tag="u3")
+        cc = const.tile([P, P], F32, name="cc", tag="cc")
+        ds_g1 = const.tile([P, 512, 4], BF16, name="ds_g1", tag="ds_g1", align_bytes=64)
+        ds_b = const.tile([P, 2048], BF16, name="ds_b", tag="ds_b", align_bytes=64)
+        ds_g2 = const.tile([P, 2048], BF16, name="ds_g2", tag="ds_g2", align_bytes=64)
+        dsc1 = const.tile([P, 512], U32, name="dsc1", tag="dsc1", align_bytes=64)
+        dss1 = const.tile([P, 512], U8, name="dss1", tag="dss1", align_bytes=64)
+        dsc2 = const.tile([P, 512], U32, name="dsc2", tag="dsc2", align_bytes=64)
+        dss2 = const.tile([P, 512], U8, name="dss2", tag="dss2", align_bytes=64)
+
+        for h in range(2):
+            s_h = scr[:, S0 + 1024 * h : S0 + 1024 * (h + 1)]
+            ta_h = scr[:, A0 + 1024 * h : A0 + 1024 * (h + 1)]
+            tb_h = scr[:, B0 + 1024 * h : B0 + 1024 * (h + 1)]
+            g_h = g_all[:, 1024 * h : 1024 * (h + 1)]
+            hs = slice(64 * h, 64 * (h + 1))
+            nc.scalar.activation(out=ta_h, in_=s_h, func=ACT.Square)
+            nc.vector.tensor_tensor(out=tb_h, in0=g_h, in1=s_h, op=ALU.mult)
+            nc.vector.tensor_reduce(
+                out=sq[:, hs], in_=ta_h.rearrange("p (g o) -> p g o", o=16), axis=AX.X, op=ALU.add
+            )
+            nc.scalar.activation(out=rt[:, hs], in_=sq[:, hs], func=ACT.Sqrt)
+            nc.vector.tensor_scalar(out=onep[:, hs], in0=sq[:, hs], scalar1=1.0, scalar2=None, op0=ALU.add)
+            nc.vector.reciprocal(out=inv[:, hs], in_=onep[:, hs])
+            nc.vector.tensor_reduce(
+                out=dot[:, hs], in_=tb_h.rearrange("p (g o) -> p g o", o=16), axis=AX.X, op=ALU.add
+            )
+            nc.vector.reciprocal(out=rinv[:, hs], in_=rt[:, hs])
+            nc.vector.tensor_tensor(out=ca[:, hs], in0=rt[:, hs], in1=inv[:, hs], op=ALU.mult)
+            nc.vector.tensor_tensor(
+                out=ta_h.rearrange("p (g o) -> p g o", o=16),
+                in0=g_h.rearrange("p (g o) -> p g o", o=16),
+                in1=ca[:, hs].unsqueeze(2).to_broadcast([P, 64, 16]),
+                op=ALU.mult,
+            )
+            nc.vector.scalar_tensor_tensor(
+                out=u1[:, hs], in0=sq[:, hs], scalar=1.0, in1=inv[:, hs], op0=ALU.subtract, op1=ALU.mult
+            )
+            nc.vector.tensor_tensor(out=u2[:, hs], in0=inv[:, hs], in1=rinv[:, hs], op=ALU.mult)
+            nc.vector.tensor_tensor(out=u3[:, hs], in0=u1[:, hs], in1=u2[:, hs], op=ALU.mult)
+            nc.vector.tensor_tensor(out=cc[:, hs], in0=u3[:, hs], in1=dot[:, hs], op=ALU.mult)
+            nc.vector.tensor_tensor(
+                out=tb_h.rearrange("p (g o) -> p g o", o=16),
+                in0=s_h.rearrange("p (g o) -> p g o", o=16),
+                in1=cc[:, hs].unsqueeze(2).to_broadcast([P, 64, 16]),
+                op=ALU.mult,
+            )
+            nc.vector.tensor_tensor(
+                out=ds_g1[:, 256 * h : 256 * (h + 1), :].rearrange("p (n o) j -> p n o j", o=16),
+                in0=ta_h.rearrange("p (n j o) -> p n o j", j=4, o=16),
+                in1=tb_h.rearrange("p (n j o) -> p n o j", j=4, o=16),
+                op=ALU.subtract,
+            )
+
+        nc.vector.quantize_mx(
+            out=dsc1[:].bitcast(E5), scales=dss1[:], in_=ds_g1[:].rearrange("p m j -> p (m j)")
+        )
+
+        def evacuate(on_vector, out, in_):
+            if on_vector:
+                nc.vector.tensor_scalar(out=out, in0=in_, scalar1=INV_R, scalar2=None, op0=ALU.mult)
+            else:
+                nc.scalar.activation(out=out, in_=in_, func=ACT.Copy, scale=INV_R)
+
+        def move(on_vector, out, in_):
+            if on_vector:
+                nc.vector.tensor_copy(out=out, in_=in_)
+            else:
+                nc.scalar.copy(out=out, in_=in_)
+
+        for c in range(2):
+            xc = cod.tile([P, KCH], U32, name="xc%d" % c, tag="codes", align_bytes=64)
+            xs = cod.tile([P, KCH], U8, name="xs%d" % c, tag="scales", align_bytes=64)
+            y = big.tile([P, 32, KL, 16], F32, name="y%d" % c, tag="big", align_bytes=64)
+            x_perm = x_raw[:, :, KCH * c : KCH * (c + 1)].rearrange("p j (kp kl) -> p kp kl j", kl=KL)
+            for lo, hi in UNITS:
+                width = (hi - lo) * 512
+                xg = rot.tile([P, 2048], BF16, name="xg", tag="rot", align_bytes=64)
+                move(
+                    c == 1 and lo >= 8,
+                    xg[:, 0:width].rearrange("p (kl kp j) -> p kp kl j", kp=P, j=4),
+                    x_perm[:, :, lo:hi],
+                )
+                nc.vector.quantize_mx(
+                    out=xc[:, P * lo : P * hi].bitcast(E4), scales=xs[:, P * lo : P * hi], in_=xg[:, 0:width]
+                )
+                for kl in range(lo, hi):
+                    ps = psum.tile([P, 512], F32, name="ps", tag="ps")
+                    nc.tensor.matmul_mx(
+                        out=ps[:],
+                        lhsT=xc[:, P * kl : P * (kl + 1)].bitcast(E4),
+                        lhsT_scale=xs[:, P * kl : P * (kl + 1)],
+                        rhs=dsc1[:].bitcast(E5),
+                        rhs_scale=dss1[:],
+                        start=True,
+                        stop=True,
+                    )
+                    on_vector = (kl % 5 in (2, 4)) if c == 0 else (kl % 4 == 3 or kl == 17)
+                    evacuate(on_vector, y[:, :, kl, :], ps[:].rearrange("p (n o) -> p n o", o=16))
+            nc.sync.dma_start(
+                out=o1f[:, 16 * KCH * c : 16 * KCH * (c + 1)].rearrange("n (kp f) -> kp n f", kp=P),
+                in_=y[:].rearrange("p n kl o -> p n (kl o)"),
+            )
+
+        for u in range(2):
+            nc.scalar.copy(
+                out=ds_b[:].rearrange("p (j u i e) -> p u j i e", u=2, i=P, e=2)[:, u],
+                in_=ds_g1[:].rearrange("p (i u e) j -> p u j i e", u=2, e=2)[:, u],
+            )
+        ds_words = ds_b[:].bitcast(F32)
+        ds_g2w = ds_g2[:].bitcast(F32).rearrange("q (j p u) -> q j p u", p=P, u=2)
+        for jh in range(2):
+            ps = psum.tile([P, 512], F32, name="ps", tag="ps")
+            for r in range(4):
+                nc.tensor.transpose(
+                    ps[:, P * r : P * (r + 1)], ds_words[:, P * (4 * jh + r) : P * (4 * jh + r + 1)], ident[:]
+                )
+            nc.scalar.copy(
+                out=ds_g2w[:, 2 * jh : 2 * jh + 2], in_=ps[:].rearrange("q (j u p) -> q j p u", u=2, p=P)
+            )
+        nc.vector.quantize_mx(out=dsc2[:].bitcast(E5), scales=dss2[:], in_=ds_g2[:])
+
+        wgr = big.tile([P, 4 * K], BF16, name="wgr", tag="big", align_bytes=64)
+        wgr_words = wgr[:].bitcast(F32).rearrange("q (kp r) -> q kp r", r=2 * WKL)
+        w_words = w_raw[:].bitcast(F32).rearrange("p (n kl q u) -> p u n kl q", kl=WKL, q=4, u=2)
+        for g in range(9):
+            wr = rot.tile([P, 1024], F32, name="wr", tag="rot", align_bytes=64)
+            for u in range(2):
+                nc.vector.tensor_copy(
+                    out=wr[:].rearrange("p (kl u n q) -> p u n kl q", u=2, n=32, q=4)[:, u],
+                    in_=w_words[:, u, :, 4 * g : 4 * (g + 1)],
+                )
+            for hb in range(2):
+                ps = psum.tile([P, 512], F32, name="ps", tag="ps")
+                for r in range(4):
+                    nc.tensor.transpose(
+                        ps[:, P * r : P * (r + 1)], wr[:, P * (4 * hb + r) : P * (4 * hb + r + 1)], ident[:]
+                    )
+                move(
+                    g % 2 == 1,
+                    wgr_words[:, :, 8 * g + 4 * hb : 8 * g + 4 * hb + 4],
+                    ps[:].rearrange("q (r kp) -> q kp r", kp=P),
+                )
+
+        for t in range(3):
+            o_tile = big.tile([P, 4, 1536], F32, name="o%d" % t, tag="big", align_bytes=64)
+            for cl in range(3):
+                c = 3 * t + cl
+                wc = wcod.tile([P, 512], U32, name="wc", tag="wc", align_bytes=64)
+                ws = wcod.tile([P, 512], U8, name="ws", tag="ws", align_bytes=64)
+                nc.vector.quantize_mx(out=wc[:].bitcast(E4), scales=ws[:], in_=wgr[:, 2048 * c : 2048 * (c + 1)])
+                for j in range(4):
+                    ps = psum.tile([P, 512], F32, name="ps", tag="ps")
+                    nc.tensor.matmul_mx(
+                        out=ps[:],
+                        lhsT=dsc2[:, P * j : P * (j + 1)].bitcast(E5),
+                        lhsT_scale=dss2[:, P * j : P * (j + 1)],
+                        rhs=wc[:].bitcast(E4),
+                        rhs_scale=ws[:],
+                        start=True,
+                        stop=True,
+                    )
+                    evacuate(j == 1 or (j == 3 and c % 2 == 0), o_tile[:, j, 512 * cl : 512 * (cl + 1)], ps[:])
+                if t == 2:
+                    nc.sync.dma_start(
+                        out=o0v[:, :, 512 * c : 512 * (c + 1)], in_=o_tile[:, :, 512 * cl : 512 * (cl + 1)]
+                    )
+            if t < 2:
+                nc.sync.dma_start(out=o0v[:, :, 1536 * t : 1536 * (t + 1)], in_=o_tile[:])

@@ -37,12 +37,13 @@ def tile_capsulelayer_v_kernel(tc, x, W, s, grad_out, out_0, out_1):
     o1f = out_1.rearrange("n r i o -> n (r i o)")
 
     with ExitStack() as ctx:
+        ctx.enter_context(tc.manual_schedule())
         const = ctx.enter_context(tc.tile_pool(name="const", bufs=1))
-        big = ctx.enter_context(tc.tile_pool(name="big", bufs=4))
+        big = ctx.enter_context(tc.tile_pool(name="big", bufs=1))
         cod = ctx.enter_context(tc.tile_pool(name="cod", bufs=2))
         wcod = ctx.enter_context(tc.tile_pool(name="wcod", bufs=3))
         rot = ctx.enter_context(tc.tile_pool(name="rot", bufs=8))
-        psum = ctx.enter_context(tc.psum_pool(name="psum", bufs=8))
+        psum = ctx.enter_context(tc.psum_pool(name="psum", bufs=4))
 
         ident = const.tile([P, P], F32, name="ident", tag="ident")
         masks.make_identity(nc, ident[:])
@@ -51,9 +52,9 @@ def tile_capsulelayer_v_kernel(tc, x, W, s, grad_out, out_0, out_1):
         nc.vector.memset(warm_in[:], 1.0)
         nc.scalar.activation(out=warm_out[:], in_=warm_in[:], func=ACT.Sqrt)
 
-        scr = big.tile([P, 9216], F32, name="scr", tag="big", align_bytes=64)
-        x_raw = big.tile([P, 4, K], BF16, name="x_raw", tag="big", align_bytes=64)
-        w_raw = big.tile([P, 32 * 576], BF16, name="w_raw", tag="big", align_bytes=64)
+        scr = big.tile([P, 9216], F32, name="scr", tag="slot_a", align_bytes=64)
+        x_raw = big.tile([P, 2, 4, KCH], BF16, name="x_raw", tag="slot_b", align_bytes=64)
+        w_raw = big.tile([P, 32 * 576], BF16, name="w_raw", tag="slot_c", align_bytes=64)
         g_all = scr[:, G0 : G0 + 1024].bitcast(BF16)
 
         def load_sg(h):
@@ -67,7 +68,7 @@ def tile_capsulelayer_v_kernel(tc, x, W, s, grad_out, out_0, out_1):
             )
 
         def load_x(c):
-            nc.sync.dma_start(out=x_raw[:, :, KCH * c : KCH * (c + 1)], in_=xv[:, :, KCH * c : KCH * (c + 1)])
+            nc.sync.dma_start(out=x_raw[:, c], in_=xv[:, :, KCH * c : KCH * (c + 1)])
 
         load_sg(0)
         load_x(0)
@@ -98,53 +99,57 @@ def tile_capsulelayer_v_kernel(tc, x, W, s, grad_out, out_0, out_1):
         dsc2 = const.tile([P, 512], U32, name="dsc2", tag="dsc2", align_bytes=64)
         dss2 = const.tile([P, 512], U8, name="dss2", tag="dss2", align_bytes=64)
 
-        for h in range(2):
-            s_h = scr[:, S0 + 1024 * h : S0 + 1024 * (h + 1)]
-            ta_h = scr[:, A0 + 1024 * h : A0 + 1024 * (h + 1)]
-            tb_h = scr[:, B0 + 1024 * h : B0 + 1024 * (h + 1)]
-            g_h = g_all[:, 1024 * h : 1024 * (h + 1)]
+        def part(base, h):
+            return scr[:, base + 1024 * h : base + 1024 * (h + 1)]
+
+        def groups(ap):
+            return ap.rearrange("p (g o) -> p g o", o=16)
+
+        def square(h):
+            nc.scalar.activation(out=part(A0, h), in_=part(S0, h), func=ACT.Square)
+
+        def root(h):
             hs = slice(64 * h, 64 * (h + 1))
-            nc.scalar.activation(out=ta_h, in_=s_h, func=ACT.Square)
-            nc.vector.tensor_tensor(out=tb_h, in0=g_h, in1=s_h, op=ALU.mult)
-            nc.vector.tensor_reduce(
-                out=sq[:, hs], in_=ta_h.rearrange("p (g o) -> p g o", o=16), axis=AX.X, op=ALU.add
-            )
             nc.scalar.activation(out=rt[:, hs], in_=sq[:, hs], func=ACT.Sqrt)
+
+        def chain_a(h):
+            hs = slice(64 * h, 64 * (h + 1))
+            g_h = g_all[:, 1024 * h : 1024 * (h + 1)]
+            nc.vector.tensor_tensor(out=part(B0, h), in0=g_h, in1=part(S0, h), op=ALU.mult)
+            nc.vector.tensor_reduce(out=sq[:, hs], in_=groups(part(A0, h)), axis=AX.X, op=ALU.add)
             nc.vector.tensor_scalar(out=onep[:, hs], in0=sq[:, hs], scalar1=1.0, scalar2=None, op0=ALU.add)
+            nc.vector.tensor_reduce(out=dot[:, hs], in_=groups(part(B0, h)), axis=AX.X, op=ALU.add)
             nc.vector.reciprocal(out=inv[:, hs], in_=onep[:, hs])
-            nc.vector.tensor_reduce(
-                out=dot[:, hs], in_=tb_h.rearrange("p (g o) -> p g o", o=16), axis=AX.X, op=ALU.add
-            )
+
+        def chain_b(h):
+            hs = slice(64 * h, 64 * (h + 1))
+            g_h = g_all[:, 1024 * h : 1024 * (h + 1)]
             nc.vector.reciprocal(out=rinv[:, hs], in_=rt[:, hs])
             nc.vector.tensor_tensor(out=ca[:, hs], in0=rt[:, hs], in1=inv[:, hs], op=ALU.mult)
-            nc.vector.tensor_tensor(
-                out=ta_h.rearrange("p (g o) -> p g o", o=16),
-                in0=g_h.rearrange("p (g o) -> p g o", o=16),
-                in1=ca[:, hs].unsqueeze(2).to_broadcast([P, 64, 16]),
-                op=ALU.mult,
-            )
             nc.vector.scalar_tensor_tensor(
                 out=u1[:, hs], in0=sq[:, hs], scalar=1.0, in1=inv[:, hs], op0=ALU.subtract, op1=ALU.mult
             )
-            nc.vector.tensor_tensor(out=u2[:, hs], in0=inv[:, hs], in1=rinv[:, hs], op=ALU.mult)
-            nc.vector.tensor_tensor(out=u3[:, hs], in0=u1[:, hs], in1=u2[:, hs], op=ALU.mult)
-            nc.vector.tensor_tensor(out=cc[:, hs], in0=u3[:, hs], in1=dot[:, hs], op=ALU.mult)
+            nc.vector.tensor_tensor(out=u2[:, hs], in0=dot[:, hs], in1=rinv[:, hs], op=ALU.mult)
+            nc.vector.tensor_tensor(out=u3[:, hs], in0=u1[:, hs], in1=inv[:, hs], op=ALU.mult)
+            nc.vector.tensor_tensor(out=cc[:, hs], in0=u2[:, hs], in1=u3[:, hs], op=ALU.mult)
             nc.vector.tensor_tensor(
-                out=tb_h.rearrange("p (g o) -> p g o", o=16),
-                in0=s_h.rearrange("p (g o) -> p g o", o=16),
+                out=groups(part(A0, h)),
+                in0=groups(g_h),
+                in1=ca[:, hs].unsqueeze(2).to_broadcast([P, 64, 16]),
+                op=ALU.mult,
+            )
+            nc.vector.tensor_tensor(
+                out=groups(part(B0, h)),
+                in0=groups(part(S0, h)),
                 in1=cc[:, hs].unsqueeze(2).to_broadcast([P, 64, 16]),
                 op=ALU.mult,
             )
             nc.vector.tensor_tensor(
                 out=ds_g1[:, 256 * h : 256 * (h + 1), :].rearrange("p (n o) j -> p n o j", o=16),
-                in0=ta_h.rearrange("p (n j o) -> p n o j", j=4, o=16),
-                in1=tb_h.rearrange("p (n j o) -> p n o j", j=4, o=16),
+                in0=part(A0, h).rearrange("p (n j o) -> p n o j", j=4, o=16),
+                in1=part(B0, h).rearrange("p (n j o) -> p n o j", j=4, o=16),
                 op=ALU.subtract,
             )
-
-        nc.vector.quantize_mx(
-            out=dsc1[:].bitcast(E5), scales=dss1[:], in_=ds_g1[:].rearrange("p m j -> p (m j)")
-        )
 
         def evacuate(on_vector, out, in_):
             if on_vector:
@@ -158,39 +163,72 @@ def tile_capsulelayer_v_kernel(tc, x, W, s, grad_out, out_0, out_1):
             else:
                 nc.scalar.copy(out=out, in_=in_)
 
+        xc = []
+        xs = []
         for c in range(2):
-            xc = cod.tile([P, KCH], U32, name="xc%d" % c, tag="codes", align_bytes=64)
-            xs = cod.tile([P, KCH], U8, name="xs%d" % c, tag="scales", align_bytes=64)
-            y = big.tile([P, 32, KL, 16], F32, name="y%d" % c, tag="big", align_bytes=64)
-            x_perm = x_raw[:, :, KCH * c : KCH * (c + 1)].rearrange("p j (kp kl) -> p kp kl j", kl=KL)
-            for lo, hi in UNITS:
-                width = (hi - lo) * 512
-                xg = rot.tile([P, 2048], BF16, name="xg", tag="rot", align_bytes=64)
-                move(
-                    c == 1 and lo >= 8,
-                    xg[:, 0:width].rearrange("p (kl kp j) -> p kp kl j", kp=P, j=4),
-                    x_perm[:, :, lo:hi],
-                )
-                nc.vector.quantize_mx(
-                    out=xc[:, P * lo : P * hi].bitcast(E4), scales=xs[:, P * lo : P * hi], in_=xg[:, 0:width]
-                )
-                for kl in range(lo, hi):
-                    ps = psum.tile([P, 512], F32, name="ps", tag="ps")
-                    nc.tensor.matmul_mx(
-                        out=ps[:],
-                        lhsT=xc[:, P * kl : P * (kl + 1)].bitcast(E4),
-                        lhsT_scale=xs[:, P * kl : P * (kl + 1)],
-                        rhs=dsc1[:].bitcast(E5),
-                        rhs_scale=dss1[:],
-                        start=True,
-                        stop=True,
-                    )
-                    on_vector = (kl % 5 in (2, 4)) if c == 0 else (kl % 4 == 3 or kl == 17)
-                    evacuate(on_vector, y[:, :, kl, :], ps[:].rearrange("p (n o) -> p n o", o=16))
+            xc.append(cod.tile([P, KCH], U32, name="xc%d" % c, tag="codes", align_bytes=64))
+            xs.append(cod.tile([P, KCH], U8, name="xs%d" % c, tag="scales", align_bytes=64))
+        xg = {}
+
+        def interleave(c, u, on_vector):
+            lo, hi = UNITS[u]
+            xg[(c, u)] = rot.tile([P, 2048], BF16, name="xg", tag="rot", align_bytes=64)
+            move(
+                on_vector,
+                xg[(c, u)][:, 0 : 512 * (hi - lo)].rearrange("p (kl kp j) -> p kp kl j", kp=P, j=4),
+                x_raw[:, c].rearrange("p j (kp kl) -> p kp kl j", kl=KL)[:, :, lo:hi],
+            )
+
+        def quantize_x(c, u):
+            lo, hi = UNITS[u]
+            nc.vector.quantize_mx(
+                out=xc[c][:, P * lo : P * hi].bitcast(E4),
+                scales=xs[c][:, P * lo : P * hi],
+                in_=xg[(c, u)][:, 0 : 512 * (hi - lo)],
+            )
+
+        def dw_pass(c, y, kl, on_vector):
+            ps = psum.tile([P, 512], F32, name="ps", tag="mm")
+            nc.tensor.matmul_mx(
+                out=ps[:],
+                lhsT=xc[c][:, P * kl : P * (kl + 1)].bitcast(E4),
+                lhsT_scale=xs[c][:, P * kl : P * (kl + 1)],
+                rhs=dsc1[:].bitcast(E5),
+                rhs_scale=dss1[:],
+                start=True,
+                stop=True,
+            )
+            evacuate(on_vector, y[:, :, kl, :], ps[:].rearrange("p (n o) -> p n o", o=16))
+
+        def store_y(c, y):
             nc.sync.dma_start(
                 out=o1f[:, 16 * KCH * c : 16 * KCH * (c + 1)].rearrange("n (kp f) -> kp n f", kp=P),
                 in_=y[:].rearrange("p n kl o -> p n (kl o)"),
             )
+
+        square(0)
+        chain_a(0)
+        root(0)
+        chain_b(0)
+        interleave(0, 0, False)
+        square(1)
+        interleave(0, 1, False)
+        chain_a(1)
+        root(1)
+        interleave(0, 2, False)
+        interleave(0, 3, False)
+        interleave(0, 4, False)
+        chain_b(1)
+        nc.vector.quantize_mx(
+            out=dsc1[:].bitcast(E5), scales=dss1[:], in_=ds_g1[:].rearrange("p m j -> p (m j)")
+        )
+
+        for u in range(5):
+            quantize_x(0, u)
+        y0 = big.tile([P, 32, KL, 16], F32, name="y0", tag="slot_d", align_bytes=64)
+        for kl in range(KL):
+            dw_pass(0, y0, kl, kl >= 4 and kl % 2 == 1)
+        store_y(0, y0)
 
         for u in range(2):
             nc.scalar.copy(
@@ -199,61 +237,92 @@ def tile_capsulelayer_v_kernel(tc, x, W, s, grad_out, out_0, out_1):
             )
         ds_words = ds_b[:].bitcast(F32)
         ds_g2w = ds_g2[:].bitcast(F32).rearrange("q (j p u) -> q j p u", p=P, u=2)
+        pd = []
         for jh in range(2):
-            ps = psum.tile([P, 512], F32, name="ps", tag="ps")
+            pd.append(psum.tile([P, 512], F32, name="pd", tag="tp"))
             for r in range(4):
                 nc.tensor.transpose(
-                    ps[:, P * r : P * (r + 1)], ds_words[:, P * (4 * jh + r) : P * (4 * jh + r + 1)], ident[:]
+                    pd[jh][:, P * r : P * (r + 1)], ds_words[:, P * (4 * jh + r) : P * (4 * jh + r + 1)], ident[:]
                 )
+        for jh in range(2):
             nc.scalar.copy(
-                out=ds_g2w[:, 2 * jh : 2 * jh + 2], in_=ps[:].rearrange("q (j u p) -> q j p u", u=2, p=P)
+                out=ds_g2w[:, 2 * jh : 2 * jh + 2], in_=pd[jh][:].rearrange("q (j u p) -> q j p u", u=2, p=P)
             )
-        nc.vector.quantize_mx(out=dsc2[:].bitcast(E5), scales=dss2[:], in_=ds_g2[:])
 
-        wgr = big.tile([P, 4 * K], BF16, name="wgr", tag="big", align_bytes=64)
+        y1 = big.tile([P, 32, KL, 16], F32, name="y1", tag="slot_a", align_bytes=64)
+        interleave(1, 0, True)
+        for u in range(5):
+            if u + 1 < 5:
+                interleave(1, u + 1, True)
+            quantize_x(1, u)
+            for kl in range(UNITS[u][0], UNITS[u][1]):
+                dw_pass(1, y1, kl, False)
+        store_y(1, y1)
+
+        wgr = big.tile([P, 4 * K], BF16, name="wgr", tag="slot_b", align_bytes=64)
         wgr_words = wgr[:].bitcast(F32).rearrange("q (kp r) -> q kp r", r=2 * WKL)
         w_words = w_raw[:].bitcast(F32).rearrange("p (n kl q u) -> p u n kl q", kl=WKL, q=4, u=2)
-        for g in range(9):
-            wr = rot.tile([P, 1024], F32, name="wr", tag="rot", align_bytes=64)
+        wr = {}
+
+        def sort_w(g):
+            wr[g] = rot.tile([P, 1024], F32, name="wr", tag="rot", align_bytes=64)
             for u in range(2):
                 nc.vector.tensor_copy(
-                    out=wr[:].rearrange("p (kl u n q) -> p u n kl q", u=2, n=32, q=4)[:, u],
+                    out=wr[g][:].rearrange("p (kl u n q) -> p u n kl q", u=2, n=32, q=4)[:, u],
                     in_=w_words[:, u, :, 4 * g : 4 * (g + 1)],
                 )
+
+        for g in range(3):
+            sort_w(g)
+        for g in range(9):
+            pw = []
             for hb in range(2):
-                ps = psum.tile([P, 512], F32, name="ps", tag="ps")
+                pw.append(psum.tile([P, 512], F32, name="pw", tag="tp"))
                 for r in range(4):
                     nc.tensor.transpose(
-                        ps[:, P * r : P * (r + 1)], wr[:, P * (4 * hb + r) : P * (4 * hb + r + 1)], ident[:]
+                        pw[hb][:, P * r : P * (r + 1)], wr[g][:, P * (4 * hb + r) : P * (4 * hb + r + 1)], ident[:]
                     )
+            if g + 3 < 9:
+                sort_w(g + 3)
+            for hb in range(2):
                 move(
-                    g % 2 == 1,
+                    g in (3, 7),
                     wgr_words[:, :, 8 * g + 4 * hb : 8 * g + 4 * hb + 4],
-                    ps[:].rearrange("q (r kp) -> q kp r", kp=P),
+                    pw[hb][:].rearrange("q (r kp) -> q kp r", kp=P),
                 )
 
-        for t in range(3):
-            o_tile = big.tile([P, 4, 1536], F32, name="o%d" % t, tag="big", align_bytes=64)
-            for cl in range(3):
-                c = 3 * t + cl
-                wc = wcod.tile([P, 512], U32, name="wc", tag="wc", align_bytes=64)
-                ws = wcod.tile([P, 512], U8, name="ws", tag="ws", align_bytes=64)
-                nc.vector.quantize_mx(out=wc[:].bitcast(E4), scales=ws[:], in_=wgr[:, 2048 * c : 2048 * (c + 1)])
-                for j in range(4):
-                    ps = psum.tile([P, 512], F32, name="ps", tag="ps")
-                    nc.tensor.matmul_mx(
-                        out=ps[:],
-                        lhsT=dsc2[:, P * j : P * (j + 1)].bitcast(E5),
-                        lhsT_scale=dss2[:, P * j : P * (j + 1)],
-                        rhs=wc[:].bitcast(E4),
-                        rhs_scale=ws[:],
-                        start=True,
-                        stop=True,
-                    )
-                    evacuate(j == 1 or (j == 3 and c % 2 == 0), o_tile[:, j, 512 * cl : 512 * (cl + 1)], ps[:])
-                if t == 2:
-                    nc.sync.dma_start(
-                        out=o0v[:, :, 512 * c : 512 * (c + 1)], in_=o_tile[:, :, 512 * cl : 512 * (cl + 1)]
-                    )
-            if t < 2:
+        nc.vector.quantize_mx(out=dsc2[:].bitcast(E5), scales=dss2[:], in_=ds_g2[:])
+        wc = {}
+        ws = {}
+
+        def quantize_w(c):
+            wc[c] = wcod.tile([P, 512], U32, name="wc", tag="wc", align_bytes=64)
+            ws[c] = wcod.tile([P, 512], U8, name="ws", tag="ws", align_bytes=64)
+            nc.vector.quantize_mx(out=wc[c][:].bitcast(E4), scales=ws[c][:], in_=wgr[:, 2048 * c : 2048 * (c + 1)])
+
+        quantize_w(0)
+        o_tile = None
+        for c in range(9):
+            t, cl = divmod(c, 3)
+            if cl == 0:
+                o_tile = big.tile([P, 4, 1536], F32, name="o%d" % t, tag=("slot_d", "slot_c", "slot_a")[t], align_bytes=64)
+            po = []
+            for j in range(4):
+                po.append(psum.tile([P, 512], F32, name="po", tag="mm"))
+                nc.tensor.matmul_mx(
+                    out=po[j][:],
+                    lhsT=dsc2[:, P * j : P * (j + 1)].bitcast(E5),
+                    lhsT_scale=dss2[:, P * j : P * (j + 1)],
+                    rhs=wc[c][:].bitcast(E4),
+                    rhs_scale=ws[c][:],
+                    start=True,
+                    stop=True,
+                )
+            if c + 1 < 9:
+                quantize_w(c + 1)
+            for j in range(4):
+                evacuate(j == 1 or (j == 3 and c % 2 == 0), o_tile[:, j, 512 * cl : 512 * (cl + 1)], po[j][:])
+            if t == 2:
+                nc.sync.dma_start(out=o0v[:, :, 512 * c : 512 * (c + 1)], in_=o_tile[:, :, 512 * cl : 512 * (cl + 1)])
+            elif cl == 2:
                 nc.sync.dma_start(out=o0v[:, :, 1536 * t : 1536 * (t + 1)], in_=o_tile[:])

@@ -19,11 +19,21 @@ P = 128
 K = 4608
 KL = 18
 KCH = P * KL
-WKL = 36
+WKL = K // P
 INV_R = 1.0 / 576.0
+
 UNITS = ((0, 4), (4, 8), (8, 12), (12, 16), (16, 18))
 
+W_GROUPS = 9
+O_CHUNKS = 9
+SORT_AHEAD = 3
+
+SLOT_F32 = 9216
+W_ROW = WKL * 16
+UNIT_COLS = 2048
+
 S0, A0, B0, G0 = 0, 2048, 4096, 6144
+HALF = 1024
 
 
 def tile_capsulelayer_v_kernel(tc, x, W, s, grad_out, out_0, out_1):
@@ -32,7 +42,7 @@ def tile_capsulelayer_v_kernel(tc, x, W, s, grad_out, out_0, out_1):
     xv = x.rearrange("(p j) r i -> p j (r i)", j=4)
     wv = W.rearrange("n r i o -> n (r i o)").rearrange("n (kp f) -> kp n f", kp=P)
     sv = s.rearrange("n (p j) o -> p n (j o)", j=4)
-    gv = grad_out.rearrange("n (p j) a c o -> p n (j a c o)", j=4)
+    gv = grad_out.rearrange("n (p j) a d o -> p n (j a d o)", j=4)
     o0v = out_0.rearrange("(p j) r i -> p j (r i)", j=4)
     o1f = out_1.rearrange("n r i o -> n (r i o)")
 
@@ -52,18 +62,18 @@ def tile_capsulelayer_v_kernel(tc, x, W, s, grad_out, out_0, out_1):
         nc.vector.memset(warm_in[:], 1.0)
         nc.scalar.activation(out=warm_out[:], in_=warm_in[:], func=ACT.Sqrt)
 
-        scr = big.tile([P, 9216], F32, name="scr", tag="slot_a", align_bytes=64)
+        scr = big.tile([P, SLOT_F32], F32, name="scr", tag="slot_a", align_bytes=64)
         x_raw = big.tile([P, 2, 4, KCH], BF16, name="x_raw", tag="slot_b", align_bytes=64)
-        w_raw = big.tile([P, 32 * 576], BF16, name="w_raw", tag="slot_c", align_bytes=64)
-        g_all = scr[:, G0 : G0 + 1024].bitcast(BF16)
+        w_raw = big.tile([P, 32 * W_ROW], BF16, name="w_raw", tag="slot_c", align_bytes=64)
+        g_all = scr[:, G0 : G0 + HALF].bitcast(BF16)
 
         def load_sg(h):
             nc.sync.dma_start(
-                out=scr[:, S0 + 1024 * h : S0 + 1024 * (h + 1)].rearrange("p (n f) -> p n f", f=64),
+                out=scr[:, S0 + HALF * h : S0 + HALF * (h + 1)].rearrange("p (n f) -> p n f", f=64),
                 in_=sv[:, 16 * h : 16 * (h + 1), :],
             )
             nc.sync.dma_start(
-                out=g_all[:, 1024 * h : 1024 * (h + 1)].rearrange("p (n f) -> p n f", f=64),
+                out=g_all[:, HALF * h : HALF * (h + 1)].rearrange("p (n f) -> p n f", f=64),
                 in_=gv[:, 16 * h : 16 * (h + 1), :],
             )
 
@@ -74,10 +84,10 @@ def tile_capsulelayer_v_kernel(tc, x, W, s, grad_out, out_0, out_1):
         load_x(0)
         load_sg(1)
         load_x(1)
-        for q in range(4):
+        for piece in range(4):
             nc.sync.dma_start(
-                out=w_raw[:, 576 * 8 * q : 576 * 8 * (q + 1)].rearrange("p (n f) -> p n f", f=576),
-                in_=wv[:, 8 * q : 8 * (q + 1), :],
+                out=w_raw[:, W_ROW * 8 * piece : W_ROW * 8 * (piece + 1)].rearrange("p (n f) -> p n f", f=W_ROW),
+                in_=wv[:, 8 * piece : 8 * (piece + 1), :],
             )
 
         sq = const.tile([P, P], F32, name="sq", tag="sq")
@@ -100,10 +110,10 @@ def tile_capsulelayer_v_kernel(tc, x, W, s, grad_out, out_0, out_1):
         dss2 = const.tile([P, 512], U8, name="dss2", tag="dss2", align_bytes=64)
 
         def part(base, h):
-            return scr[:, base + 1024 * h : base + 1024 * (h + 1)]
+            return scr[:, base + HALF * h : base + HALF * (h + 1)]
 
         def groups(ap):
-            return ap.rearrange("p (g o) -> p g o", o=16)
+            return ap.rearrange("p (nj o) -> p nj o", o=16)
 
         def square(h):
             nc.scalar.activation(out=part(A0, h), in_=part(S0, h), func=ACT.Square)
@@ -114,7 +124,7 @@ def tile_capsulelayer_v_kernel(tc, x, W, s, grad_out, out_0, out_1):
 
         def chain_a(h):
             hs = slice(64 * h, 64 * (h + 1))
-            g_h = g_all[:, 1024 * h : 1024 * (h + 1)]
+            g_h = g_all[:, HALF * h : HALF * (h + 1)]
             nc.vector.tensor_tensor(out=part(B0, h), in0=g_h, in1=part(S0, h), op=ALU.mult)
             nc.vector.tensor_reduce(out=sq[:, hs], in_=groups(part(A0, h)), axis=AX.X, op=ALU.add)
             nc.vector.tensor_scalar(out=onep[:, hs], in0=sq[:, hs], scalar1=1.0, scalar2=None, op0=ALU.add)
@@ -123,7 +133,7 @@ def tile_capsulelayer_v_kernel(tc, x, W, s, grad_out, out_0, out_1):
 
         def chain_b(h):
             hs = slice(64 * h, 64 * (h + 1))
-            g_h = g_all[:, 1024 * h : 1024 * (h + 1)]
+            g_h = g_all[:, HALF * h : HALF * (h + 1)]
             nc.vector.reciprocal(out=rinv[:, hs], in_=rt[:, hs])
             nc.vector.tensor_tensor(out=ca[:, hs], in0=rt[:, hs], in1=inv[:, hs], op=ALU.mult)
             nc.vector.scalar_tensor_tensor(
@@ -170,21 +180,21 @@ def tile_capsulelayer_v_kernel(tc, x, W, s, grad_out, out_0, out_1):
             xs.append(cod.tile([P, KCH], U8, name="xs%d" % c, tag="scales", align_bytes=64))
         xg = {}
 
-        def interleave(c, u, on_vector):
-            lo, hi = UNITS[u]
-            xg[(c, u)] = rot.tile([P, 2048], BF16, name="xg", tag="rot", align_bytes=64)
+        def interleave(c, unit, on_vector):
+            lo, hi = UNITS[unit]
+            xg[(c, unit)] = rot.tile([P, UNIT_COLS], BF16, name="xg", tag="rot", align_bytes=64)
             move(
                 on_vector,
-                xg[(c, u)][:, 0 : 512 * (hi - lo)].rearrange("p (kl kp j) -> p kp kl j", kp=P, j=4),
+                xg[(c, unit)][:, 0 : 512 * (hi - lo)].rearrange("p (kl kp j) -> p kp kl j", kp=P, j=4),
                 x_raw[:, c].rearrange("p j (kp kl) -> p kp kl j", kl=KL)[:, :, lo:hi],
             )
 
-        def quantize_x(c, u):
-            lo, hi = UNITS[u]
+        def quantize_x(c, unit):
+            lo, hi = UNITS[unit]
             nc.vector.quantize_mx(
                 out=xc[c][:, P * lo : P * hi].bitcast(E4),
                 scales=xs[c][:, P * lo : P * hi],
-                in_=xg[(c, u)][:, 0 : 512 * (hi - lo)],
+                in_=xg[(c, unit)][:, 0 : 512 * (hi - lo)],
             )
 
         def dw_pass(c, y, kl, on_vector):
@@ -201,10 +211,12 @@ def tile_capsulelayer_v_kernel(tc, x, W, s, grad_out, out_0, out_1):
             evacuate(on_vector, y[:, :, kl, :], ps[:].rearrange("p (n o) -> p n o", o=16))
 
         def store_y(c, y):
-            nc.sync.dma_start(
-                out=o1f[:, 16 * KCH * c : 16 * KCH * (c + 1)].rearrange("n (kp f) -> kp n f", kp=P),
-                in_=y[:].rearrange("p n kl o -> p n (kl o)"),
-            )
+            for piece in range(4):
+                caps = slice(8 * piece, 8 * (piece + 1))
+                nc.sync.dma_start(
+                    out=o1f[caps, 16 * KCH * c : 16 * KCH * (c + 1)].rearrange("n (kp f) -> kp n f", kp=P),
+                    in_=y[:, caps].rearrange("p n kl o -> p n (kl o)"),
+                )
 
         square(0)
         chain_a(0)
@@ -223,8 +235,8 @@ def tile_capsulelayer_v_kernel(tc, x, W, s, grad_out, out_0, out_1):
             out=dsc1[:].bitcast(E5), scales=dss1[:], in_=ds_g1[:].rearrange("p m j -> p (m j)")
         )
 
-        for u in range(5):
-            quantize_x(0, u)
+        for unit in range(len(UNITS)):
+            quantize_x(0, unit)
         y0 = big.tile([P, 32, KL, 16], F32, name="y0", tag="slot_d", align_bytes=64)
         for kl in range(KL):
             dw_pass(0, y0, kl, kl >= 4 and kl % 2 == 1)
@@ -232,97 +244,113 @@ def tile_capsulelayer_v_kernel(tc, x, W, s, grad_out, out_0, out_1):
 
         for u in range(2):
             nc.scalar.copy(
-                out=ds_b[:].rearrange("p (j u i e) -> p u j i e", u=2, i=P, e=2)[:, u],
-                in_=ds_g1[:].rearrange("p (i u e) j -> p u j i e", u=2, e=2)[:, u],
+                out=ds_b[:].rearrange("p (j u pm e) -> p u j pm e", u=2, pm=P, e=2)[:, u],
+                in_=ds_g1[:].rearrange("p (pm u e) j -> p u j pm e", u=2, e=2)[:, u],
             )
         ds_words = ds_b[:].bitcast(F32)
-        ds_g2w = ds_g2[:].bitcast(F32).rearrange("q (j p u) -> q j p u", p=P, u=2)
+        ds_g2w = ds_g2[:].bitcast(F32).rearrange("pm (j p u) -> pm j p u", p=P, u=2)
         pd = []
         for jh in range(2):
             pd.append(psum.tile([P, 512], F32, name="pd", tag="tp"))
-            for r in range(4):
+            for quarter in range(4):
                 nc.tensor.transpose(
-                    pd[jh][:, P * r : P * (r + 1)], ds_words[:, P * (4 * jh + r) : P * (4 * jh + r + 1)], ident[:]
+                    pd[jh][:, P * quarter : P * (quarter + 1)],
+                    ds_words[:, P * (4 * jh + quarter) : P * (4 * jh + quarter + 1)],
+                    ident[:],
                 )
         for jh in range(2):
             nc.scalar.copy(
-                out=ds_g2w[:, 2 * jh : 2 * jh + 2], in_=pd[jh][:].rearrange("q (j u p) -> q j p u", u=2, p=P)
+                out=ds_g2w[:, 2 * jh : 2 * jh + 2], in_=pd[jh][:].rearrange("pm (j u p) -> pm j p u", u=2, p=P)
             )
 
         y1 = big.tile([P, 32, KL, 16], F32, name="y1", tag="slot_a", align_bytes=64)
         interleave(1, 0, True)
-        for u in range(5):
-            if u + 1 < 5:
-                interleave(1, u + 1, True)
-            quantize_x(1, u)
-            for kl in range(UNITS[u][0], UNITS[u][1]):
+        for unit in range(len(UNITS)):
+            if unit + 1 < len(UNITS):
+                interleave(1, unit + 1, True)
+            quantize_x(1, unit)
+            for kl in range(UNITS[unit][0], UNITS[unit][1]):
                 dw_pass(1, y1, kl, False)
         store_y(1, y1)
 
         wgr = big.tile([P, 4 * K], BF16, name="wgr", tag="slot_b", align_bytes=64)
-        wgr_words = wgr[:].bitcast(F32).rearrange("q (kp r) -> q kp r", r=2 * WKL)
-        w_words = w_raw[:].bitcast(F32).rearrange("p (n kl q u) -> p u n kl q", kl=WKL, q=4, u=2)
+        wgr_words = wgr[:].bitcast(F32).rearrange("pm (kp w) -> pm kp w", w=2 * WKL)
+        w_words = w_raw[:].bitcast(F32).rearrange("kp (n kl q u) -> kp u n kl q", kl=WKL, q=4, u=2)
         wr = {}
 
-        def sort_w(g):
-            wr[g] = rot.tile([P, 1024], F32, name="wr", tag="rot", align_bytes=64)
+        def sort_w(grp):
+            wr[grp] = rot.tile([P, UNIT_COLS // 2], F32, name="wr", tag="rot", align_bytes=64)
             for u in range(2):
                 nc.vector.tensor_copy(
-                    out=wr[g][:].rearrange("p (kl u n q) -> p u n kl q", u=2, n=32, q=4)[:, u],
-                    in_=w_words[:, u, :, 4 * g : 4 * (g + 1)],
+                    out=wr[grp][:].rearrange("kp (kl u n q) -> kp u n kl q", u=2, n=32, q=4)[:, u],
+                    in_=w_words[:, u, :, 4 * grp : 4 * (grp + 1)],
                 )
 
-        for g in range(3):
-            sort_w(g)
-        for g in range(9):
+        for grp in range(SORT_AHEAD):
+            sort_w(grp)
+        for grp in range(W_GROUPS):
             pw = []
             for hb in range(2):
                 pw.append(psum.tile([P, 512], F32, name="pw", tag="tp"))
-                for r in range(4):
+                for quarter in range(4):
                     nc.tensor.transpose(
-                        pw[hb][:, P * r : P * (r + 1)], wr[g][:, P * (4 * hb + r) : P * (4 * hb + r + 1)], ident[:]
+                        pw[hb][:, P * quarter : P * (quarter + 1)],
+                        wr[grp][:, P * (4 * hb + quarter) : P * (4 * hb + quarter + 1)],
+                        ident[:],
                     )
-            if g + 3 < 9:
-                sort_w(g + 3)
+            if grp + SORT_AHEAD < W_GROUPS:
+                sort_w(grp + SORT_AHEAD)
             for hb in range(2):
                 move(
-                    g in (3, 7),
-                    wgr_words[:, :, 8 * g + 4 * hb : 8 * g + 4 * hb + 4],
-                    pw[hb][:].rearrange("q (r kp) -> q kp r", kp=P),
+                    grp in (3, 7),
+                    wgr_words[:, :, 8 * grp + 4 * hb : 8 * grp + 4 * hb + 4],
+                    pw[hb][:].rearrange("pm (quarter kp) -> pm kp quarter", kp=P),
                 )
 
         nc.vector.quantize_mx(out=dsc2[:].bitcast(E5), scales=dss2[:], in_=ds_g2[:])
         wc = {}
         ws = {}
 
-        def quantize_w(c):
-            wc[c] = wcod.tile([P, 512], U32, name="wc", tag="wc", align_bytes=64)
-            ws[c] = wcod.tile([P, 512], U8, name="ws", tag="ws", align_bytes=64)
-            nc.vector.quantize_mx(out=wc[c][:].bitcast(E4), scales=ws[c][:], in_=wgr[:, 2048 * c : 2048 * (c + 1)])
+        def quantize_w(oc):
+            wc[oc] = wcod.tile([P, 512], U32, name="wc", tag="wc", align_bytes=64)
+            ws[oc] = wcod.tile([P, 512], U8, name="ws", tag="ws", align_bytes=64)
+            nc.vector.quantize_mx(
+                out=wc[oc][:].bitcast(E4), scales=ws[oc][:], in_=wgr[:, 2048 * oc : 2048 * (oc + 1)]
+            )
 
         quantize_w(0)
-        o_tile = None
-        for c in range(9):
-            t, cl = divmod(c, 3)
-            if cl == 0:
-                o_tile = big.tile([P, 4, 1536], F32, name="o%d" % t, tag=("slot_d", "slot_c", "slot_a")[t], align_bytes=64)
-            po = []
-            for j in range(4):
-                po.append(psum.tile([P, 512], F32, name="po", tag="mm"))
-                nc.tensor.matmul_mx(
-                    out=po[j][:],
-                    lhsT=dsc2[:, P * j : P * (j + 1)].bitcast(E5),
-                    lhsT_scale=dss2[:, P * j : P * (j + 1)],
-                    rhs=wc[c][:].bitcast(E4),
-                    rhs_scale=ws[c][:],
-                    start=True,
-                    stop=True,
-                )
-            if c + 1 < 9:
-                quantize_w(c + 1)
-            for j in range(4):
-                evacuate(j == 1 or (j == 3 and c % 2 == 0), o_tile[:, j, 512 * cl : 512 * (cl + 1)], po[j][:])
-            if t == 2:
-                nc.sync.dma_start(out=o0v[:, :, 512 * c : 512 * (c + 1)], in_=o_tile[:, :, 512 * cl : 512 * (cl + 1)])
-            elif cl == 2:
-                nc.sync.dma_start(out=o0v[:, :, 1536 * t : 1536 * (t + 1)], in_=o_tile[:])
+        for tile_no in range(3):
+            o_tile = big.tile(
+                [P, 4, 1536],
+                F32,
+                name="o%d" % tile_no,
+                tag=("slot_d", "slot_c", "slot_a")[tile_no],
+                align_bytes=64,
+            )
+            for third in range(3):
+                oc = 3 * tile_no + third
+                po = []
+                for j in range(4):
+                    po.append(psum.tile([P, 512], F32, name="po", tag="mm"))
+                    nc.tensor.matmul_mx(
+                        out=po[j][:],
+                        lhsT=dsc2[:, P * j : P * (j + 1)].bitcast(E5),
+                        lhsT_scale=dss2[:, P * j : P * (j + 1)],
+                        rhs=wc[oc][:].bitcast(E4),
+                        rhs_scale=ws[oc][:],
+                        start=True,
+                        stop=True,
+                    )
+                if oc + 1 < O_CHUNKS:
+                    quantize_w(oc + 1)
+                for j in range(4):
+                    evacuate(
+                        j == 1 or (j == 3 and oc % 2 == 0), o_tile[:, j, 512 * third : 512 * (third + 1)], po[j][:]
+                    )
+                if tile_no == 2:
+                    nc.sync.dma_start(
+                        out=o0v[:, :, 512 * oc : 512 * (oc + 1)], in_=o_tile[:, :, 512 * third : 512 * (third + 1)]
+                    )
+                elif third == 2:
+                    for j in range(4):
+                        nc.sync.dma_start(out=o0v[:, j, 1536 * tile_no : 1536 * (tile_no + 1)], in_=o_tile[:, j, :])

@@ -269,8 +269,8 @@ def tile_capsulelayer_v_kernel(tc, x, W, s, grad_out, out_0, out_1):
             if unit + 1 < len(UNITS):
                 interleave(1, unit + 1, True)
             quantize_x(1, unit)
-            for kl in range(UNITS[unit][0], UNITS[unit][1]):
-                dw_pass(1, y1, kl, False)
+        for kl in range(KL):
+            dw_pass(1, y1, kl, kl >= 10 and kl % 2 == 1)
         store_y(1, y1)
 
         wgr = big.tile([P, 4 * K], BF16, name="wgr", tag="slot_b", align_bytes=64)
@@ -347,10 +347,6 @@ def tile_capsulelayer_v_kernel(tc, x, W, s, grad_out, out_0, out_1):
                     evacuate(
                         j == 1 or (j == 3 and oc % 2 == 0), o_tile[:, j, 512 * third : 512 * (third + 1)], po[j][:]
                     )
-                if tile_no == 2:
-                    nc.sync.dma_start(
-                        out=o0v[:, :, 512 * oc : 512 * (oc + 1)], in_=o_tile[:, :, 512 * third : 512 * (third + 1)]
-                    )
-                elif third == 2:
-                    for j in range(4):
-                        nc.sync.dma_start(out=o0v[:, j, 1536 * tile_no : 1536 * (tile_no + 1)], in_=o_tile[:, j, :])
+                nc.sync.dma_start(
+                    out=o0v[:, :, 512 * oc : 512 * (oc + 1)], in_=o_tile[:, :, 512 * third : 512 * (third + 1)]
+                )

from contextlib import ExitStack

import concourse.masks as masks
import concourse.mybir as mybir

FLOPS = 2 * 2 * 512 * 4608 * 512

F32 = mybir.dt.float32
BF16 = mybir.dt.bfloat16
U32 = mybir.dt.uint32
U8 = mybir.dt.uint8
E4 = mybir.dt.float8_e4m3fn_x4
E5 = mybir.dt.float8_e5m2_x4
ALU = mybir.AluOpType
ACT = mybir.ActivationFunctionType
AX = mybir.AxisListType

P = 128
K = 4608
KL = 18
KCH = P * KL
WKL = K // P
INV_R = 1.0 / 576.0

UNITS = ((0, 4), (4, 8), (8, 12), (12, 16), (16, 18))

W_GROUPS = 9
O_CHUNKS = 9
SORT_AHEAD = 3

SLOT_F32 = 9216
W_ROW = WKL * 16
UNIT_COLS = 2048

S0, A0, B0, G0 = 0, 2048, 4096, 6144
HALF = 1024


def tile_capsulelayer_v_kernel(tc, x, W, s, grad_out, out_0, out_1):
    nc = tc.nc

    xv = x.rearrange("(p j) r i -> p j (r i)", j=4)
    wv = W.rearrange("n r i o -> n (r i o)").rearrange("n (kp f) -> kp n f", kp=P)
    sv = s.rearrange("n (p j) o -> p n (j o)", j=4)
    gv = grad_out.rearrange("n (p j) a d o -> p n (j a d o)", j=4)
    o0v = out_0.rearrange("(p j) r i -> p j (r i)", j=4)
    o1f = out_1.rearrange("n r i o -> n (r i o)")

    with ExitStack() as ctx:
        ctx.enter_context(tc.manual_schedule())
        const = ctx.enter_context(tc.tile_pool(name="const", bufs=1))
        big = ctx.enter_context(tc.tile_pool(name="big", bufs=1))
        cod = ctx.enter_context(tc.tile_pool(name="cod", bufs=2))
        wcod = ctx.enter_context(tc.tile_pool(name="wcod", bufs=3))
        rot = ctx.enter_context(tc.tile_pool(name="rot", bufs=8))
        psum = ctx.enter_context(tc.psum_pool(name="psum", bufs=4))

        ident = const.tile([P, P], F32, name="ident", tag="ident")
        masks.make_identity(nc, ident[:])
        warm_in = const.tile([P, 8], F32, name="warm_in", tag="warm_in")
        warm_out = const.tile([P, 8], F32, name="warm_out", tag="warm_out")
        nc.vector.memset(warm_in[:], 1.0)
        nc.scalar.activation(out=warm_out[:], in_=warm_in[:], func=ACT.Sqrt)

        scr = big.tile([P, SLOT_F32], F32, name="scr", tag="slot_a", align_bytes=64)
        x_raw = big.tile([P, 2, 4, KCH], BF16, name="x_raw", tag="slot_b", align_bytes=64)
        w_raw = big.tile([P, 32 * W_ROW], BF16, name="w_raw", tag="slot_c", align_bytes=64)
        g_all = scr[:, G0 : G0 + HALF].bitcast(BF16)

        def load_sg(h):
            nc.sync.dma_start(
                out=scr[:, S0 + HALF * h : S0 + HALF * (h + 1)].rearrange("p (n f) -> p n f", f=64),
                in_=sv[:, 16 * h : 16 * (h + 1), :],
            )
            nc.sync.dma_start(
                out=g_all[:, HALF * h : HALF * (h + 1)].rearrange("p (n f) -> p n f", f=64),
                in_=gv[:, 16 * h : 16 * (h + 1), :],
            )

        def load_x(c):
            nc.sync.dma_start(out=x_raw[:, c], in_=xv[:, :, KCH * c : KCH * (c + 1)])

        load_sg(0)
        load_x(0)
        load_sg(1)
        load_x(1)
        for piece in range(4):
            nc.sync.dma_start(
                out=w_raw[:, W_ROW * 8 * piece : W_ROW * 8 * (piece + 1)].rearrange("p (n f) -> p n f", f=W_ROW),
                in_=wv[:, 8 * piece : 8 * (piece + 1), :],
            )

        sq = const.tile([P, P], F32, name="sq", tag="sq")
        dot = const.tile([P, P], F32, name="dot", tag="dot")
        rt = const.tile([P, P], F32, name="rt", tag="rt")
        onep = const.tile([P, P], F32, name="onep", tag="onep")
        inv = const.tile([P, P], F32, name="inv", tag="inv")
        rinv = const.tile([P, P], F32, name="rinv", tag="rinv")
        ca = const.tile([P, P], F32, name="ca", tag="ca")
        u1 = const.tile([P, P], F32, name="u1", tag="u1")
        u2 = const.tile([P, P], F32, name="u2", tag="u2")
        u3 = const.tile([P, P], F32, name="u3", tag="u3")
        cc = const.tile([P, P], F32, name="cc", tag="cc")
        ds_g1 = const.tile([P, 512, 4], BF16, name="ds_g1", tag="ds_g1", align_bytes=64)
        ds_b = const.tile([P, 2048], BF16, name="ds_b", tag="ds_b", align_bytes=64)
        ds_g2 = const.tile([P, 2048], BF16, name="ds_g2", tag="ds_g2", align_bytes=64)
        dsc1 = const.tile([P, 512], U32, name="dsc1", tag="dsc1", align_bytes=64)
        dss1 = const.tile([P, 512], U8, name="dss1", tag="dss1", align_bytes=64)
        dsc2 = const.tile([P, 512], U32, name="dsc2", tag="dsc2", align_bytes=64)
        dss2 = const.tile([P, 512], U8, name="dss2", tag="dss2", align_bytes=64)

        def part(base, h):
            return scr[:, base + HALF * h : base + HALF * (h + 1)]

        def groups(ap):
            return ap.rearrange("p (nj o) -> p nj o", o=16)

        def square(h):
            nc.scalar.activation(out=part(A0, h), in_=part(S0, h), func=ACT.Square)

        def root(h):
            hs = slice(64 * h, 64 * (h + 1))
            nc.scalar.activation(out=rt[:, hs], in_=sq[:, hs], func=ACT.Sqrt)

        def chain_a(h):
            hs = slice(64 * h, 64 * (h + 1))
            g_h = g_all[:, HALF * h : HALF * (h + 1)]
            nc.vector.tensor_tensor(out=part(B0, h), in0=g_h, in1=part(S0, h), op=ALU.mult)
            nc.vector.tensor_reduce(out=sq[:, hs], in_=groups(part(A0, h)), axis=AX.X, op=ALU.add)
            nc.vector.tensor_scalar(out=onep[:, hs], in0=sq[:, hs], scalar1=1.0, scalar2=None, op0=ALU.add)
            nc.vector.tensor_reduce(out=dot[:, hs], in_=groups(part(B0, h)), axis=AX.X, op=ALU.add)
            nc.vector.reciprocal(out=inv[:, hs], in_=onep[:, hs])

        def chain_b(h):
            hs = slice(64 * h, 64 * (h + 1))
            g_h = g_all[:, HALF * h : HALF * (h + 1)]
            nc.vector.reciprocal(out=rinv[:, hs], in_=rt[:, hs])
            nc.vector.tensor_tensor(out=ca[:, hs], in0=rt[:, hs], in1=inv[:, hs], op=ALU.mult)
            nc.vector.scalar_tensor_tensor(
                out=u1[:, hs], in0=sq[:, hs], scalar=1.0, in1=inv[:, hs], op0=ALU.subtract, op1=ALU.mult
            )
            nc.vector.tensor_tensor(out=u2[:, hs], in0=dot[:, hs], in1=rinv[:, hs], op=ALU.mult)
            nc.vector.tensor_tensor(out=u3[:, hs], in0=u1[:, hs], in1=inv[:, hs], op=ALU.mult)
            nc.vector.tensor_tensor(out=cc[:, hs], in0=u2[:, hs], in1=u3[:, hs], op=ALU.mult)
            nc.vector.tensor_tensor(
                out=groups(part(A0, h)),
                in0=groups(g_h),
                in1=ca[:, hs].unsqueeze(2).to_broadcast([P, 64, 16]),
                op=ALU.mult,
            )
            nc.vector.tensor_tensor(
                out=groups(part(B0, h)),
                in0=groups(part(S0, h)),
                in1=cc[:, hs].unsqueeze(2).to_broadcast([P, 64, 16]),
                op=ALU.mult,
            )
            nc.vector.tensor_tensor(
                out=ds_g1[:, 256 * h : 256 * (h + 1), :].rearrange("p (n o) j -> p n o j", o=16),
                in0=part(A0, h).rearrange("p (n j o) -> p n o j", j=4, o=16),
                in1=part(B0, h).rearrange("p (n j o) -> p n o j", j=4, o=16),
                op=ALU.subtract,
            )

        def evacuate(on_vector, out, in_):
            if on_vector:
                nc.vector.tensor_scalar(out=out, in0=in_, scalar1=INV_R, scalar2=None, op0=ALU.mult)
            else:
                nc.scalar.activation(out=out, in_=in_, func=ACT.Copy, scale=INV_R)

        def move(on_vector, out, in_):
            if on_vector:
                nc.vector.tensor_copy(out=out, in_=in_)
            else:
                nc.scalar.copy(out=out, in_=in_)

        xc = []
        xs = []
        for c in range(2):
            xc.append(cod.tile([P, KCH], U32, name="xc%d" % c, tag="codes", align_bytes=64))
            xs.append(cod.tile([P, KCH], U8, name="xs%d" % c, tag="scales", align_bytes=64))
        xg = {}

        def interleave(c, unit, on_vector):
            lo, hi = UNITS[unit]
            xg[(c, unit)] = rot.tile([P, UNIT_COLS], BF16, name="xg", tag="rot", align_bytes=64)
            move(
                on_vector,
                xg[(c, unit)][:, 0 : 512 * (hi - lo)].rearrange("p (kl kp j) -> p kp kl j", kp=P, j=4),
                x_raw[:, c].rearrange("p j (kp kl) -> p kp kl j", kl=KL)[:, :, lo:hi],
            )

        def quantize_x(c, unit):
            lo, hi = UNITS[unit]
            nc.vector.quantize_mx(
                out=xc[c][:, P * lo : P * hi].bitcast(E4),
                scales=xs[c][:, P * lo : P * hi],
                in_=xg[(c, unit)][:, 0 : 512 * (hi - lo)],
            )

        def dw_pass(c, y, kl, on_vector):
            ps = psum.tile([P, 512], F32, name="ps", tag="mm")
            nc.tensor.matmul_mx(
                out=ps[:],
                lhsT=xc[c][:, P * kl : P * (kl + 1)].bitcast(E4),
                lhsT_scale=xs[c][:, P * kl : P * (kl + 1)],
                rhs=dsc1[:].bitcast(E5),
                rhs_scale=dss1[:],
                start=True,
                stop=True,
            )
            evacuate(on_vector, y[:, :, kl, :], ps[:].rearrange("p (n o) -> p n o", o=16))

        def store_y(c, y):
            for piece in range(4):
                caps = slice(8 * piece, 8 * (piece + 1))
                nc.sync.dma_start(
                    out=o1f[caps, 16 * KCH * c : 16 * KCH * (c + 1)].rearrange("n (kp f) -> kp n f", kp=P),
                    in_=y[:, caps].rearrange("p n kl o -> p n (kl o)"),
                )

        square(0)
        chain_a(0)
        root(0)
        chain_b(0)
        interleave(0, 0, False)
        square(1)
        interleave(0, 1, False)
        chain_a(1)
        root(1)
        interleave(0, 2, False)
        interleave(0, 3, False)
        interleave(0, 4, False)
        chain_b(1)
        nc.vector.quantize_mx(
            out=dsc1[:].bitcast(E5), scales=dss1[:], in_=ds_g1[:].rearrange("p m j -> p (m j)")
        )

        for unit in range(len(UNITS)):
            quantize_x(0, unit)
        y0 = big.tile([P, 32, KL, 16], F32, name="y0", tag="slot_d", align_bytes=64)
        for kl in range(KL):
            dw_pass(0, y0, kl, kl >= 4 and kl % 2 == 1)
        store_y(0, y0)

        for u in range(2):
            nc.scalar.copy(
                out=ds_b[:].rearrange("p (j u pm e) -> p u j pm e", u=2, pm=P, e=2)[:, u],
                in_=ds_g1[:].rearrange("p (pm u e) j -> p u j pm e", u=2, e=2)[:, u],
            )
        ds_words = ds_b[:].bitcast(F32)
        ds_g2w = ds_g2[:].bitcast(F32).rearrange("pm (j p u) -> pm j p u", p=P, u=2)
        pd = []
        for jh in range(2):
            pd.append(psum.tile([P, 512], F32, name="pd", tag="tp"))
            for quarter in range(4):
                nc.tensor.transpose(
                    pd[jh][:, P * quarter : P * (quarter + 1)],
                    ds_words[:, P * (4 * jh + quarter) : P * (4 * jh + quarter + 1)],
                    ident[:],
                )
        for jh in range(2):
            nc.scalar.copy(
                out=ds_g2w[:, 2 * jh : 2 * jh + 2], in_=pd[jh][:].rearrange("pm (j u p) -> pm j p u", u=2, p=P)
            )

        y1 = big.tile([P, 32, KL, 16], F32, name="y1", tag="slot_a", align_bytes=64)
        interleave(1, 0, True)
        for unit in range(len(UNITS)):
            if unit + 1 < len(UNITS):
                interleave(1, unit + 1, True)
            quantize_x(1, unit)
        for kl in range(KL):
            dw_pass(1, y1, kl, kl >= 10 and kl % 2 == 1)
        store_y(1, y1)

        wgr = big.tile([P, 4 * K], BF16, name="wgr", tag="slot_b", align_bytes=64)
        wgr_words = wgr[:].bitcast(F32).rearrange("pm (kp w) -> pm kp w", w=2 * WKL)
        w_words = w_raw[:].bitcast(F32).rearrange("kp (n kl q u) -> kp u n kl q", kl=WKL, q=4, u=2)
        wr = {}

        def sort_w(grp):
            wr[grp] = rot.tile([P, UNIT_COLS // 2], F32, name="wr", tag="rot", align_bytes=64)
            for u in range(2):
                nc.vector.tensor_copy(
                    out=wr[grp][:].rearrange("kp (kl u n q) -> kp u n kl q", u=2, n=32, q=4)[:, u],
                    in_=w_words[:, u, :, 4 * grp : 4 * (grp + 1)],
                )

        for grp in range(SORT_AHEAD):
            sort_w(grp)
        for grp in range(W_GROUPS):
            pw = []
            for hb in range(2):
                pw.append(psum.tile([P, 512], F32, name="pw", tag="tp"))
                for quarter in range(4):
                    nc.tensor.transpose(
                        pw[hb][:, P * quarter : P * (quarter + 1)],
                        wr[grp][:, P * (4 * hb + quarter) : P * (4 * hb + quarter + 1)],
                        ident[:],
                    )
            if grp + SORT_AHEAD < W_GROUPS:
                sort_w(grp + SORT_AHEAD)
            for hb in range(2):
                move(
                    grp in (3, 7),
                    wgr_words[:, :, 8 * grp + 4 * hb : 8 * grp + 4 * hb + 4],
                    pw[hb][:].rearrange("pm (quarter kp) -> pm kp quarter", kp=P),
                )

        nc.vector.quantize_mx(out=dsc2[:].bitcast(E5), scales=dss2[:], in_=ds_g2[:])
        wc = {}
        ws = {}

        def quantize_w(oc):
            wc[oc] = wcod.tile([P, 512], U32, name="wc", tag="wc", align_bytes=64)
            ws[oc] = wcod.tile([P, 512], U8, name="ws", tag="ws", align_bytes=64)
            nc.vector.quantize_mx(
                out=wc[oc][:].bitcast(E4), scales=ws[oc][:], in_=wgr[:, 2048 * oc : 2048 * (oc + 1)]
            )

        quantize_w(0)
        for tile_no in range(3):
            o_tile = big.tile(
                [P, 4, 1536],
                F32,
                name="o%d" % tile_no,
                tag=("slot_d", "slot_c", "slot_a")[tile_no],
                align_bytes=64,
            )
            for third in range(3):
                oc = 3 * tile_no + third
                po = []
                for j in range(4):
                    po.append(psum.tile([P, 512], F32, name="po", tag="mm"))
                    nc.tensor.matmul_mx(
                        out=po[j][:],
                        lhsT=dsc2[:, P * j : P * (j + 1)].bitcast(E5),
                        lhsT_scale=dss2[:, P * j : P * (j + 1)],
                        rhs=wc[oc][:].bitcast(E4),
                        rhs_scale=ws[oc][:],
                        start=True,
                        stop=True,
                    )
                if oc + 1 < O_CHUNKS:
                    quantize_w(oc + 1)
                for j in range(4):
                    evacuate(
                        j == 1 or (j == 3 and oc % 2 == 0), o_tile[:, j, 512 * third : 512 * (third + 1)], po[j][:]
                    )
                nc.sync.dma_start(
                    out=o0v[:, :, 512 * oc : 512 * (oc + 1)], in_=o_tile[:, :, 512 * third : 512 * (third + 1)]
                )
